import numpy as np
import ml_dtypes


def mxq(x, axis, fmt="e4m3"):
    dtype, down = {"e4m3": (ml_dtypes.float8_e4m3fn, 7), "e5m2": (ml_dtypes.float8_e5m2, 14)}[fmt]
    v = np.moveaxis(np.asarray(x, np.float32).astype(ml_dtypes.bfloat16).astype(np.float64), axis, -1)
    blocks = v.reshape(v.shape[:-1] + (-1, 32))
    amax = np.abs(blocks).max(-1, keepdims=True)
    byte = np.maximum(np.where(amax > 0, np.frexp(amax)[1] - 1 + 127, 0) - down, 1)
    scale = np.exp2(byte - 127.0)
    codes = (blocks / scale).astype(np.float32).astype(dtype).astype(np.float64)
    return np.moveaxis((codes * scale).reshape(v.shape), -1, axis)


WIDE = False


def mx_kscale(k):
    if not WIDE:
        return np.ones(k)
    levels = np.array([10, -10, 5, -5, 0])
    if k % 512:
        return np.exp2(np.random.permutation(np.resize(levels, k // 32))).repeat(32)
    a = np.empty((k // 512, 16))
    for p in range(k // 512):
        a[p, :8] = np.random.permutation(np.resize(levels, 8))
        for g in range(8):
            far = levels[np.abs(levels - a[p, g]) >= 10]
            a[p, g + 8] = far[np.random.randint(len(far))]
    return np.exp2(a.ravel()).repeat(32)


BF16 = ml_dtypes.bfloat16


def bf(x):
    return np.asarray(x, np.float32).astype(BF16)


def f64(x):
    return np.asarray(x).astype(np.float64)


B, S, D, P, PW, L = 2, 192, 512, 4, 2, 2


def sigmoid(v):
    return 1.0 / (1.0 + np.exp(-v))


def setup_inputs():
    n = np.random.standard_normal
    s = mx_kscale(D)
    return {"x": bf(n((B, S, D)) * s),
            "amp_w": bf(n((D, D)) / np.sqrt(D) / s[:, None]),
            "amp_b": bf(n(D) * 0.3),
            "ph_w": bf(n((D, D)) / np.sqrt(D) / s[:, None]),
            "ph_b": bf(n(D) * 0.3)}


def reference(x, amp_w, amp_b, ph_w, ph_b):
    xq = mxq(f64(x), 2, "e4m3")
    amp = sigmoid((xq @ mxq(f64(amp_w), 0, "e4m3")) + f64(amp_b))
    ph = np.tanh((xq @ mxq(f64(ph_w), 0, "e4m3")) + f64(ph_b)) * np.pi
    return (np.cos(ph) + np.sin(ph)) * amp

@@ -1,0 +1,208 @@
+import math
+from contextlib import ExitStack
+
+import concourse.mybir as mybir
+from concourse.masks import make_identity
+
+F32 = mybir.dt.float32
+BF16 = mybir.dt.bfloat16
+U32 = mybir.dt.uint32
+U8 = mybir.dt.uint8
+FP8X4 = mybir.dt.float8_e4m3fn_x4
+ACT = mybir.ActivationFunctionType
+ALU = mybir.AluOpType
+
+P = 128
+PACK = 4
+K = P * PACK
+TOKENS = 384
+TOKEN_TILES = TOKENS // P
+FEATURES = 512
+FEATURE_TILES = FEATURES // P
+HALF = 256
+
+FLOPS = 2 * TOKENS * K * 2 * FEATURES
+
+
+def tile_of(f):
+    return slice(f * P, (f + 1) * P)
+
+
+def load_weight(nc, pool, weight, name):
+    raw = pool.tile([P, PACK, FEATURES], BF16, name=name)
+    nc.sync.dma_start(
+        out=raw[:].rearrange("q t n -> q (t n)"),
+        in_=weight.rearrange("(q t) n -> q (t n)", t=PACK),
+    )
+    return raw
+
+
+def quantise(nc, codes, scales, grouped, cols):
+    nc.vector.quantize_mx(
+        out=codes[:, cols].bitcast(FP8X4),
+        scales=scales[:, cols],
+        in_=grouped[:, cols, :].rearrange("p c t -> p (c t)"),
+    )
+
+
+def quantise_weight(nc, pool, raw, name):
+    grouped = pool.tile([P, FEATURES, PACK], BF16, name=name + "_grouped", align_bytes=64)
+    codes = pool.tile([P, FEATURES], U32, name=name + "_codes", align_bytes=64)
+    scales = pool.tile([P, FEATURES], U8, name=name + "_scales", align_bytes=64)
+    halves = (slice(0, HALF), slice(HALF, FEATURES))
+    for cols in halves:
+        nc.vector.tensor_copy(
+            out=grouped[:, cols, :].rearrange("p (c i) t -> p c t i", i=4),
+            in_=raw[:, :, cols].rearrange("p t (c i) -> p c t i", i=4),
+        )
+    for cols in halves:
+        quantise(nc, codes, scales, grouped, cols)
+    return codes, scales
+
+
+def multiply(nc, banks, w_codes, w_scales, x_codes, x_scales, f, name):
+    product = banks.tile([P, TOKENS], F32, tag="bank", name=name)
+    for tokens in (slice(0, HALF), slice(HALF, TOKENS)):
+        nc.tensor.matmul_mx(
+            out=product[:, tokens],
+            lhsT=w_codes[:, tile_of(f)].bitcast(FP8X4),
+            lhsT_scale=w_scales[:, tile_of(f)],
+            rhs=x_codes[:, tokens].bitcast(FP8X4),
+            rhs_scale=x_scales[:, tokens],
+            start=True,
+            stop=True,
+        )
+    return product
+
+
+def to_token_rows(nc, banks, values, ident, name):
+    transposed = banks.tile([P, TOKEN_TILES, P], F32, tag="bank", name=name)
+    for a in range(TOKEN_TILES):
+        nc.tensor.transpose(transposed[:, a, :], values[:, tile_of(a)], ident[:])
+    return transposed
+
+
+def tile_quantuminspiredneuralcore_pa_s_kernel(tc, x, amp_w, amp_b, ph_w, ph_b, out):
+    nc = tc.nc
+    x_rows = x.flatten_outer_dims().rearrange("(p a) k -> p a k", a=TOKEN_TILES)
+    out_rows = out.flatten_outer_dims().rearrange("(p a) n -> p a n", a=TOKEN_TILES)
+
+    with ExitStack() as stack:
+        keep = stack.enter_context(tc.tile_pool(name="keep", bufs=1))
+        banks = stack.enter_context(tc.psum_pool(name="banks", bufs=8))
+        stack.enter_context(tc.manual_schedule())
+
+        ph_raw = load_weight(nc, keep, ph_w, "ph_raw")
+        x_sb = keep.tile([P, TOKEN_TILES, K], BF16)
+        for a in range(TOKEN_TILES):
+            nc.sync.dma_start(out=x_sb[:, a, :], in_=x_rows[:, a, :])
+        amp_raw = load_weight(nc, keep, amp_w, "amp_raw")
+        bias_rows = keep.tile([P, P], BF16)
+        nc.vector.memset(bias_rows[:], 0.0)
+        nc.scalar.dma_start(
+            out=bias_rows[0:FEATURE_TILES, :], in_=amp_b.rearrange("(f c) -> f c", c=P)
+        )
+        nc.scalar.dma_start(
+            out=bias_rows[FEATURE_TILES : 2 * FEATURE_TILES, :],
+            in_=ph_b.rearrange("(f c) -> f c", c=P),
+        )
+
+        ident_f32 = keep.tile([P, P], F32)
+        make_identity(nc, ident_f32[:])
+        ident_bf16 = keep.tile([P, P], BF16)
+        make_identity(nc, ident_bf16[:])
+        one = keep.tile([P, 1], F32)
+        nc.vector.memset(one[:], 1.0)
+        unused = keep.tile([P, 1], F32)
+        nc.scalar.activation(out=unused[:], in_=one[:], func=ACT.Silu)
+
+        ph_codes, ph_scales = quantise_weight(nc, keep, ph_raw, "ph")
+
+        x_words = x_sb[:].bitcast(F32).rearrange("p a (q u) -> p a u q", u=2)
+        x_grouped = keep.tile([P, TOKENS, PACK], BF16, align_bytes=64)
+        x_grouped_words = x_grouped[:].bitcast(F32)
+        for a in range(TOKEN_TILES):
+            x_t = banks.tile([P, 2, P], F32, tag="bank", name="x_t")
+            for u in range(2):
+                nc.tensor.transpose(x_t[:, u, :], x_words[:, a, u, :], ident_f32[:])
+            nc.scalar.copy(
+                out=x_grouped_words[:, tile_of(a), :], in_=x_t[:].rearrange("q u c -> q c u")
+            )
+        x_codes = keep.tile([P, TOKENS], U32, align_bytes=64)
+        x_scales = keep.tile([P, TOKENS], U8, align_bytes=64)
+        quantise(nc, x_codes, x_scales, x_grouped, slice(0, HALF))
+        quantise(nc, x_codes, x_scales, x_grouped, slice(HALF, TOKENS))
+
+        bias_t = banks.tile([P, P], BF16, tag="bank", name="bias_t")
+        nc.tensor.transpose(bias_t[:], bias_rows[:], ident_bf16[:])
+        half_amp_bias = keep.tile([P, FEATURE_TILES], F32)
+        nc.scalar.mul(out=half_amp_bias[:], in_=bias_t[:, 0:FEATURE_TILES], mul=0.5)
+        ph_bias = keep.tile([P, FEATURE_TILES], F32)
+        nc.scalar.copy(out=ph_bias[:], in_=bias_t[:, FEATURE_TILES : 2 * FEATURE_TILES])
+
+        tanh_ph = keep.tile([P, FEATURE_TILES, TOKENS], F32)
+        for f in range(FEATURE_TILES):
+            product = multiply(nc, banks, ph_codes, ph_scales, x_codes, x_scales, f, "ph_product")
+            nc.scalar.activation(
+                out=tanh_ph[:, f, :], in_=product[:], func=ACT.Tanh, bias=ph_bias[:, f : f + 1]
+            )
+
+        amp_codes, amp_scales = quantise_weight(nc, keep, amp_raw, "amp")
+        tanh_amp = keep.tile([P, FEATURE_TILES, TOKENS], F32)
+        for f in range(FEATURE_TILES):
+            product = multiply(nc, banks, amp_codes, amp_scales, x_codes, x_scales, f, "amp_product")
+            nc.scalar.activation(
+                out=tanh_amp[:, f, :],
+                in_=product[:],
+                func=ACT.Tanh,
+                bias=half_amp_bias[:, f : f + 1],
+                scale=0.5,
+            )
+
+        mirrored = keep.tile([P, FEATURE_TILES, TOKENS], F32)
+        folded = keep.tile([P, FEATURE_TILES, TOKENS], F32)
+        gain = keep.tile([P, FEATURE_TILES, TOKENS], F32)
+        folded_t = []
+        gain_t = []
+        for step in range(FEATURE_TILES + 2):
+            if step < FEATURE_TILES:
+                f = step
+                nc.vector.tensor_scalar(
+                    out=mirrored[:, f, :],
+                    in0=tanh_ph[:, f, :],
+                    scalar1=-1.0,
+                    scalar2=0.75,
+                    op0=ALU.mult,
+                    op1=ALU.add,
+                )
+            if 1 <= step <= FEATURE_TILES:
+                f = step - 1
+                nc.vector.scalar_tensor_tensor(
+                    out=folded[:, f, :],
+                    in0=tanh_ph[:, f, :],
+                    scalar=0.25,
+                    in1=mirrored[:, f, :],
+                    op0=ALU.add,
+                    op1=ALU.min,
+                )
+                folded_t.append(to_token_rows(nc, banks, folded[:, f, :], ident_f32, "folded_t"))
+            if step >= 2:
+                f = step - 2
+                nc.vector.tensor_scalar(
+                    out=gain[:, f, :],
+                    in0=tanh_amp[:, f, :],
+                    scalar1=1.0,
+                    scalar2=1.0 / math.sqrt(2.0),
+                    op0=ALU.add,
+                    op1=ALU.mult,
+                )
+                gain_t.append(to_token_rows(nc, banks, gain[:, f, :], ident_f32, "gain_t"))
+
+        sine = keep.tile([P, FEATURE_TILES, TOKEN_TILES, P], F32)
+        result = keep.tile([P, TOKEN_TILES, FEATURES], F32)
+        for f in range(FEATURE_TILES):
+            nc.scalar.activation(out=sine[:, f], in_=folded_t[f][:], func=ACT.Sin, scale=math.pi)
+            nc.vector.tensor_tensor(
+                out=result[:, :, tile_of(f)], in0=sine[:, f], in1=gain_t[f][:], op=ALU.mult
+            )
+            nc.sync.dma_start(out=out_rows[:, :, tile_of(f)], in_=result[:, :, tile_of(f)])

@@ -28,16 +28,14 @@ def tile_of(f):
     return slice(f * P, (f + 1) * P)
 
 
-def load_weight(nc, pool, weight, name):
-    raw = pool.tile([P, PACK, FEATURES], BF16, name=name)
+def load_weight(nc, raw, weight, cols):
     nc.sync.dma_start(
-        out=raw[:].rearrange("q t n -> q (t n)"),
-        in_=weight.rearrange("(q t) n -> q (t n)", t=PACK),
+        out=raw[:, :, cols], in_=weight.rearrange("(q t) n -> q t n", t=PACK)[:, :, cols]
     )
-    return raw
 
 
-def quantise(nc, codes, scales, grouped, cols):
+def quantise(nc, op, cols):
+    grouped, codes, scales = op
     nc.vector.quantize_mx(
         out=codes[:, cols].bitcast(FP8X4),
         scales=scales[:, cols],
@@ -45,41 +43,40 @@ def quantise(nc, codes, scales, grouped, cols):
     )
 
 
-def quantise_weight(nc, pool, raw, name):
-    grouped = pool.tile([P, FEATURES, PACK], BF16, name=name + "_grouped", align_bytes=64)
-    codes = pool.tile([P, FEATURES], U32, name=name + "_codes", align_bytes=64)
-    scales = pool.tile([P, FEATURES], U8, name=name + "_scales", align_bytes=64)
-    halves = (slice(0, HALF), slice(HALF, FEATURES))
-    for cols in halves:
-        nc.vector.tensor_copy(
-            out=grouped[:, cols, :].rearrange("p (c i) t -> p c t i", i=4),
-            in_=raw[:, :, cols].rearrange("p t (c i) -> p c t i", i=4),
-        )
-    for cols in halves:
-        quantise(nc, codes, scales, grouped, cols)
-    return codes, scales
+def group(copy, op, raw, cols):
+    copy(
+        out=op[0][:, cols, :].rearrange("p (c i) t -> p c t i", i=4),
+        in_=raw[:, :, cols].rearrange("p t (c i) -> p c t i", i=4),
+    )
 
 
-def multiply(nc, banks, w_codes, w_scales, x_codes, x_scales, f, name):
+def operand(pool, columns, name):
+    grouped = pool.tile([P, columns, PACK], BF16, name=name + "_grouped", align_bytes=64)
+    codes = pool.tile([P, columns], U32, name=name + "_codes", align_bytes=64)
+    scales = pool.tile([P, columns], U8, name=name + "_scales", align_bytes=64)
+    return grouped, codes, scales
+
+
+def multiply(nc, banks, w, x, f, name):
     product = banks.tile([P, TOKENS], F32, tag="bank", name=name)
     for tokens in (slice(0, HALF), slice(HALF, TOKENS)):
         nc.tensor.matmul_mx(
             out=product[:, tokens],
-            lhsT=w_codes[:, tile_of(f)].bitcast(FP8X4),
-            lhsT_scale=w_scales[:, tile_of(f)],
-            rhs=x_codes[:, tokens].bitcast(FP8X4),
-            rhs_scale=x_scales[:, tokens],
+            lhsT=w[1][:, tile_of(f)].bitcast(FP8X4),
+            lhsT_scale=w[2][:, tile_of(f)],
+            rhs=x[1][:, tokens].bitcast(FP8X4),
+            rhs_scale=x[2][:, tokens],
             start=True,
             stop=True,
         )
     return product
 
 
-def to_token_rows(nc, banks, values, ident, name):
-    transposed = banks.tile([P, TOKEN_TILES, P], F32, tag="bank", name=name)
-    for a in range(TOKEN_TILES):
-        nc.tensor.transpose(transposed[:, a, :], values[:, tile_of(a)], ident[:])
-    return transposed
+def to_token_rows(nc, banks, values, ident, tiles, name):
+    rows = banks.tile([P, len(tiles), P], F32, tag="bank", name=name)
+    for i in range(len(tiles)):
+        nc.tensor.transpose(rows[:, i, :], values[:, tile_of(tiles[i])], ident[:])
+    return rows
 
 
 def tile_quantuminspiredneuralcore_pa_s_kernel(tc, x, amp_w, amp_b, ph_w, ph_b, out):
@@ -92,20 +89,25 @@ def tile_quantuminspiredneuralcore_pa_s_kernel(tc, x, amp_w, amp_b, ph_w, ph_b, 
         banks = stack.enter_context(tc.psum_pool(name="banks", bufs=8))
         stack.enter_context(tc.manual_schedule())
 
-        ph_raw = load_weight(nc, keep, ph_w, "ph_raw")
         x_sb = keep.tile([P, TOKEN_TILES, K], BF16)
         for a in range(TOKEN_TILES):
             nc.sync.dma_start(out=x_sb[:, a, :], in_=x_rows[:, a, :])
-        amp_raw = load_weight(nc, keep, amp_w, "amp_raw")
+        ph_raw = keep.tile([P, PACK, FEATURES], BF16)
+        amp_raw = keep.tile([P, PACK, FEATURES], BF16)
         bias_rows = keep.tile([P, P], BF16)
         nc.vector.memset(bias_rows[:], 0.0)
-        nc.scalar.dma_start(
+        zeros = keep.tile([P, P], F32)
+        nc.vector.memset(zeros[:], 0.0)
+        load_weight(nc, ph_raw, ph_w, slice(0, HALF))
+        nc.sync.dma_start(
             out=bias_rows[0:FEATURE_TILES, :], in_=amp_b.rearrange("(f c) -> f c", c=P)
         )
-        nc.scalar.dma_start(
+        nc.sync.dma_start(
             out=bias_rows[FEATURE_TILES : 2 * FEATURE_TILES, :],
             in_=ph_b.rearrange("(f c) -> f c", c=P),
         )
+        load_weight(nc, ph_raw, ph_w, slice(HALF, FEATURES))
+        load_weight(nc, amp_raw, amp_w, slice(0, FEATURES))
 
         ident_f32 = keep.tile([P, P], F32)
         make_identity(nc, ident_f32[:])
@@ -116,11 +118,17 @@ def tile_quantuminspiredneuralcore_pa_s_kernel(tc, x, amp_w, amp_b, ph_w, ph_b, 
         unused = keep.tile([P, 1], F32)
         nc.scalar.activation(out=unused[:], in_=one[:], func=ACT.Silu)
 
-        ph_codes, ph_scales = quantise_weight(nc, keep, ph_raw, "ph")
+        idle = banks.tile([P, P], F32, tag="bank", name="idle")
+
+        def keep_warm(count, columns):
+            for i in range(count):
+                nc.tensor.matmul(idle[:, 0:columns], lhsT=zeros[:], rhs=zeros[:, 0:columns], start=True, stop=True)
+
+        keep_warm(3, 128)
 
         x_words = x_sb[:].bitcast(F32).rearrange("p a (q u) -> p a u q", u=2)
-        x_grouped = keep.tile([P, TOKENS, PACK], BF16, align_bytes=64)
-        x_grouped_words = x_grouped[:].bitcast(F32)
+        x_op = operand(keep, TOKENS, "x")
+        x_grouped_words = x_op[0][:].bitcast(F32)
         for a in range(TOKEN_TILES):
             x_t = banks.tile([P, 2, P], F32, tag="bank", name="x_t")
             for u in range(2):
@@ -128,10 +136,6 @@ def tile_quantuminspiredneuralcore_pa_s_kernel(tc, x, amp_w, amp_b, ph_w, ph_b, 
             nc.scalar.copy(
                 out=x_grouped_words[:, tile_of(a), :], in_=x_t[:].rearrange("q u c -> q c u")
             )
-        x_codes = keep.tile([P, TOKENS], U32, align_bytes=64)
-        x_scales = keep.tile([P, TOKENS], U8, align_bytes=64)
-        quantise(nc, x_codes, x_scales, x_grouped, slice(0, HALF))
-        quantise(nc, x_codes, x_scales, x_grouped, slice(HALF, TOKENS))
 
         bias_t = banks.tile([P, P], BF16, tag="bank", name="bias_t")
         nc.tensor.transpose(bias_t[:], bias_rows[:], ident_bf16[:])
@@ -139,70 +143,104 @@ def tile_quantuminspiredneuralcore_pa_s_kernel(tc, x, amp_w, amp_b, ph_w, ph_b, 
         nc.scalar.mul(out=half_amp_bias[:], in_=bias_t[:, 0:FEATURE_TILES], mul=0.5)
         ph_bias = keep.tile([P, FEATURE_TILES], F32)
         nc.scalar.copy(out=ph_bias[:], in_=bias_t[:, FEATURE_TILES : 2 * FEATURE_TILES])
+        keep_warm(4, 64)
+
+        ph_op = operand(keep, FEATURES, "ph")
+        amp_op = operand(keep, FEATURES, "amp")
+        last = FEATURE_TILES - 1
+        group(nc.scalar.copy, ph_op, ph_raw, tile_of(last))
+        group(nc.vector.tensor_copy, ph_op, ph_raw, tile_of(0))
+        group(nc.vector.tensor_copy, ph_op, ph_raw, tile_of(1))
+        quantise(nc, x_op, slice(0, HALF))
+        quantise(nc, ph_op, tile_of(0))
+        quantise(nc, x_op, slice(HALF, TOKENS))
+        quantise(nc, ph_op, tile_of(1))
+        group(nc.vector.tensor_copy, ph_op, ph_raw, tile_of(2))
+        quantise(nc, ph_op, tile_of(last))
+        quantise(nc, ph_op, tile_of(2))
+        group(nc.vector.tensor_copy, amp_op, amp_raw, tile_of(0))
+        for f in range(1, FEATURE_TILES):
+            group(nc.vector.tensor_copy, amp_op, amp_raw, tile_of(f))
+            quantise(nc, amp_op, tile_of(f - 1))
+        quantise(nc, amp_op, tile_of(last))
 
         tanh_ph = keep.tile([P, FEATURE_TILES, TOKENS], F32)
-        for f in range(FEATURE_TILES):
-            product = multiply(nc, banks, ph_codes, ph_scales, x_codes, x_scales, f, "ph_product")
+        tanh_amp = keep.tile([P, FEATURE_TILES, TOKENS], F32)
+        sine = keep.tile([P, FEATURE_TILES, TOKEN_TILES, P], F32)
+        square = keep.tile([P, FEATURE_TILES, TOKEN_TILES, P], F32)
+        wave = keep.tile([P, FEATURE_TILES, TOKEN_TILES, P], F32)
+        result = keep.tile([P, TOKEN_TILES, FEATURES], F32)
+
+        for f in (0, 1, 3, 2):
+            product = multiply(nc, banks, ph_op, x_op, f, "ph_product")
             nc.scalar.activation(
                 out=tanh_ph[:, f, :], in_=product[:], func=ACT.Tanh, bias=ph_bias[:, f : f + 1]
             )
 
-        amp_codes, amp_scales = quantise_weight(nc, keep, amp_raw, "amp")
-        tanh_amp = keep.tile([P, FEATURE_TILES, TOKENS], F32)
-        for f in range(FEATURE_TILES):
-            product = multiply(nc, banks, amp_codes, amp_scales, x_codes, x_scales, f, "amp_product")
+        every = range(TOKEN_TILES)
+        ph_rows = {}
+        products = {}
+
+        def turn_ph(f):
+            ph_rows[f] = to_token_rows(nc, banks, tanh_ph[:, f, :], ident_f32, every, "tanh_ph_t")
+
+        def take_sine(f):
             nc.scalar.activation(
-                out=tanh_amp[:, f, :],
-                in_=product[:],
+                out=sine[:, f], in_=ph_rows[f][:], func=ACT.Sin, scale=0.5 * math.pi, bias=-0.125 * math.pi
+            )
+            nc.vector.scalar_tensor_tensor(
+                out=square[:, f], in0=sine[:, f], scalar=math.sqrt(2.0), in1=sine[:, f], op0=ALU.mult, op1=ALU.mult
+            )
+
+        def take_wave(f, engine):
+            engine.tensor_scalar(
+                out=wave[:, f], in0=square[:, f], scalar1=-1.0, scalar2=1.0 / math.sqrt(2.0), op0=ALU.mult, op1=ALU.add
+            )
+
+        def multiply_amp(f):
+            products[f] = multiply(nc, banks, amp_op, x_op, f, "amp_product")
+
+        def take_tanh(f, tiles):
+            tokens = slice(tiles[0] * P, (tiles[-1] + 1) * P)
+            nc.scalar.activation(
+                out=tanh_amp[:, f, tokens],
+                in_=products[f][:, tokens],
                 func=ACT.Tanh,
                 bias=half_amp_bias[:, f : f + 1],
                 scale=0.5,
             )
 
-        mirrored = keep.tile([P, FEATURE_TILES, TOKENS], F32)
-        folded = keep.tile([P, FEATURE_TILES, TOKENS], F32)
-        gain = keep.tile([P, FEATURE_TILES, TOKENS], F32)
-        folded_t = []
-        gain_t = []
-        for step in range(FEATURE_TILES + 2):
-            if step < FEATURE_TILES:
-                f = step
-                nc.vector.tensor_scalar(
-                    out=mirrored[:, f, :],
-                    in0=tanh_ph[:, f, :],
-                    scalar1=-1.0,
-                    scalar2=0.75,
-                    op0=ALU.mult,
-                    op1=ALU.add,
-                )
-            if 1 <= step <= FEATURE_TILES:
-                f = step - 1
-                nc.vector.scalar_tensor_tensor(
-                    out=folded[:, f, :],
-                    in0=tanh_ph[:, f, :],
-                    scalar=0.25,
-                    in1=mirrored[:, f, :],
-                    op0=ALU.add,
-                    op1=ALU.min,
-                )
-                folded_t.append(to_token_rows(nc, banks, folded[:, f, :], ident_f32, "folded_t"))
-            if step >= 2:
-                f = step - 2
-                nc.vector.tensor_scalar(
-                    out=gain[:, f, :],
-                    in0=tanh_amp[:, f, :],
-                    scalar1=1.0,
-                    scalar2=1.0 / math.sqrt(2.0),
-                    op0=ALU.add,
-                    op1=ALU.mult,
-                )
-                gain_t.append(to_token_rows(nc, banks, gain[:, f, :], ident_f32, "gain_t"))
-
-        sine = keep.tile([P, FEATURE_TILES, TOKEN_TILES, P], F32)
-        result = keep.tile([P, TOKEN_TILES, FEATURES], F32)
-        for f in range(FEATURE_TILES):
-            nc.scalar.activation(out=sine[:, f], in_=folded_t[f][:], func=ACT.Sin, scale=math.pi)
-            nc.vector.tensor_tensor(
-                out=result[:, :, tile_of(f)], in0=sine[:, f], in1=gain_t[f][:], op=ALU.mult
+        def finish(f, tiles):
+            part = slice(tiles[0], tiles[-1] + 1)
+            rows = to_token_rows(nc, banks, tanh_amp[:, f, :], ident_f32, tiles, "tanh_amp_t")
+            nc.vector.scalar_tensor_tensor(
+                out=result[:, part, tile_of(f)], in0=rows[:], scalar=1.0, in1=wave[:, f, part, :], op0=ALU.add, op1=ALU.mult
             )
-            nc.sync.dma_start(out=out_rows[:, :, tile_of(f)], in_=result[:, :, tile_of(f)])
+            nc.sync.dma_start(out=out_rows[:, part, tile_of(f)], in_=result[:, part, tile_of(f)])
+
+        turn_ph(0)
+        turn_ph(1)
+        turn_ph(3)
+        turn_ph(2)
+        take_sine(0)
+        take_wave(0, nc.gpsimd)
+        take_sine(1)
+        take_wave(1, nc.gpsimd)
+        multiply_amp(0)
+        take_sine(3)
+        multiply_amp(1)
+        take_tanh(0, every)
+        take_wave(3, nc.vector)
+        take_sine(2)
+        multiply_amp(2)
+        multiply_amp(3)
+        take_tanh(1, every)
+        finish(0, every)
+        take_wave(2, nc.vector)
+        take_tanh(2, every)
+        finish(1, every)
+        take_tanh(3, range(0, 2))
+        finish(2, every)
+        finish(3, range(0, 2))
+        take_tanh(3, range(2, TOKEN_TILES))
+        finish(3, range(2, TOKEN_TILES))

@@ -57,18 +57,22 @@ def operand(pool, columns, name):
     return grouped, codes, scales
 
 
-def multiply(nc, banks, w, x, f, name):
+def multiply(nc, out, w, x, f, tokens):
+    nc.tensor.matmul_mx(
+        out=out,
+        lhsT=w[1][:, tile_of(f)].bitcast(FP8X4),
+        lhsT_scale=w[2][:, tile_of(f)],
+        rhs=x[1][:, tokens].bitcast(FP8X4),
+        rhs_scale=x[2][:, tokens],
+        start=True,
+        stop=True,
+    )
+
+
+def multiply_all(nc, banks, w, x, f, name):
     product = banks.tile([P, TOKENS], F32, tag="bank", name=name)
     for tokens in (slice(0, HALF), slice(HALF, TOKENS)):
-        nc.tensor.matmul_mx(
-            out=product[:, tokens],
-            lhsT=w[1][:, tile_of(f)].bitcast(FP8X4),
-            lhsT_scale=w[2][:, tile_of(f)],
-            rhs=x[1][:, tokens].bitcast(FP8X4),
-            rhs_scale=x[2][:, tokens],
-            start=True,
-            stop=True,
-        )
+        multiply(nc, product[:, tokens], w, x, f, tokens)
     return product
 
 
@@ -137,28 +141,29 @@ def tile_quantuminspiredneuralcore_pa_s_kernel(tc, x, amp_w, amp_b, ph_w, ph_b, 
                 out=x_grouped_words[:, tile_of(a), :], in_=x_t[:].rearrange("q u c -> q c u")
             )
 
+        keep_warm(3, 64)
+
         bias_t = banks.tile([P, P], BF16, tag="bank", name="bias_t")
         nc.tensor.transpose(bias_t[:], bias_rows[:], ident_bf16[:])
-        half_amp_bias = keep.tile([P, FEATURE_TILES], F32)
-        nc.scalar.mul(out=half_amp_bias[:], in_=bias_t[:, 0:FEATURE_TILES], mul=0.5)
-        ph_bias = keep.tile([P, FEATURE_TILES], F32)
-        nc.scalar.copy(out=ph_bias[:], in_=bias_t[:, FEATURE_TILES : 2 * FEATURE_TILES])
-        keep_warm(4, 64)
 
         ph_op = operand(keep, FEATURES, "ph")
         amp_op = operand(keep, FEATURES, "amp")
         last = FEATURE_TILES - 1
         group(nc.scalar.copy, ph_op, ph_raw, tile_of(last))
+        half_amp_bias = keep.tile([P, FEATURE_TILES], F32)
+        nc.scalar.mul(out=half_amp_bias[:], in_=bias_t[:, 0:FEATURE_TILES], mul=0.5)
+        ph_bias = keep.tile([P, FEATURE_TILES], F32)
+        nc.scalar.copy(out=ph_bias[:], in_=bias_t[:, FEATURE_TILES : 2 * FEATURE_TILES])
         group(nc.vector.tensor_copy, ph_op, ph_raw, tile_of(0))
         group(nc.vector.tensor_copy, ph_op, ph_raw, tile_of(1))
-        quantise(nc, x_op, slice(0, HALF))
         quantise(nc, ph_op, tile_of(0))
-        quantise(nc, x_op, slice(HALF, TOKENS))
+        for a in range(TOKEN_TILES):
+            quantise(nc, x_op, tile_of(a))
         quantise(nc, ph_op, tile_of(1))
         group(nc.vector.tensor_copy, ph_op, ph_raw, tile_of(2))
         quantise(nc, ph_op, tile_of(last))
-        quantise(nc, ph_op, tile_of(2))
         group(nc.vector.tensor_copy, amp_op, amp_raw, tile_of(0))
+        quantise(nc, ph_op, tile_of(2))
         for f in range(1, FEATURE_TILES):
             group(nc.vector.tensor_copy, amp_op, amp_raw, tile_of(f))
             quantise(nc, amp_op, tile_of(f - 1))
@@ -171,8 +176,14 @@ def tile_quantuminspiredneuralcore_pa_s_kernel(tc, x, amp_w, amp_b, ph_w, ph_b, 
         wave = keep.tile([P, FEATURE_TILES, TOKEN_TILES, P], F32)
         result = keep.tile([P, TOKEN_TILES, FEATURES], F32)
 
-        for f in (0, 1, 3, 2):
-            product = multiply(nc, banks, ph_op, x_op, f, "ph_product")
+        for a in range(TOKEN_TILES):
+            product = banks.tile([P, P], F32, tag="bank", name="ph_part")
+            multiply(nc, product[:], ph_op, x_op, 0, tile_of(a))
+            nc.scalar.activation(
+                out=tanh_ph[:, 0, tile_of(a)], in_=product[:], func=ACT.Tanh, bias=ph_bias[:, 0:1]
+            )
+        for f in (1, 3, 2):
+            product = multiply_all(nc, banks, ph_op, x_op, f, "ph_product")
             nc.scalar.activation(
                 out=tanh_ph[:, f, :], in_=product[:], func=ACT.Tanh, bias=ph_bias[:, f : f + 1]
             )
@@ -198,7 +209,7 @@ def tile_quantuminspiredneuralcore_pa_s_kernel(tc, x, amp_w, amp_b, ph_w, ph_b, 
             )
 
         def multiply_amp(f):
-            products[f] = multiply(nc, banks, amp_op, x_op, f, "amp_product")
+            products[f] = multiply_all(nc, banks, amp_op, x_op, f, "amp_product")
 
         def take_tanh(f, tiles):
             tokens = slice(tiles[0] * P, (tiles[-1] + 1) * P)

@@ -150,15 +150,14 @@ def tile_quantuminspiredneuralcore_pa_s_kernel(tc, x, amp_w, amp_b, ph_w, ph_b, 
         amp_op = operand(keep, FEATURES, "amp")
         last = FEATURE_TILES - 1
         group(nc.scalar.copy, ph_op, ph_raw, tile_of(last))
-        half_amp_bias = keep.tile([P, FEATURE_TILES], F32)
-        nc.scalar.mul(out=half_amp_bias[:], in_=bias_t[:, 0:FEATURE_TILES], mul=0.5)
         ph_bias = keep.tile([P, FEATURE_TILES], F32)
         nc.scalar.copy(out=ph_bias[:], in_=bias_t[:, FEATURE_TILES : 2 * FEATURE_TILES])
         group(nc.vector.tensor_copy, ph_op, ph_raw, tile_of(0))
         group(nc.vector.tensor_copy, ph_op, ph_raw, tile_of(1))
         quantise(nc, ph_op, tile_of(0))
-        for a in range(TOKEN_TILES):
-            quantise(nc, x_op, tile_of(a))
+        x_parts = (slice(0, HALF), slice(HALF, TOKENS))
+        for tokens in x_parts:
+            quantise(nc, x_op, tokens)
         quantise(nc, ph_op, tile_of(1))
         group(nc.vector.tensor_copy, ph_op, ph_raw, tile_of(2))
         quantise(nc, ph_op, tile_of(last))
@@ -176,11 +175,12 @@ def tile_quantuminspiredneuralcore_pa_s_kernel(tc, x, amp_w, amp_b, ph_w, ph_b, 
         wave = keep.tile([P, FEATURE_TILES, TOKEN_TILES, P], F32)
         result = keep.tile([P, TOKEN_TILES, FEATURES], F32)
 
-        for a in range(TOKEN_TILES):
-            product = banks.tile([P, P], F32, tag="bank", name="ph_part")
-            multiply(nc, product[:], ph_op, x_op, 0, tile_of(a))
+        for tokens in x_parts:
+            product = banks.tile([P, HALF], F32, tag="bank", name="ph_part")
+            columns = tokens.stop - tokens.start
+            multiply(nc, product[:, 0:columns], ph_op, x_op, 0, tokens)
             nc.scalar.activation(
-                out=tanh_ph[:, 0, tile_of(a)], in_=product[:], func=ACT.Tanh, bias=ph_bias[:, 0:1]
+                out=tanh_ph[:, 0, tokens], in_=product[:, 0:columns], func=ACT.Tanh, bias=ph_bias[:, 0:1]
             )
         for f in (1, 3, 2):
             product = multiply_all(nc, banks, ph_op, x_op, f, "ph_product")
@@ -237,6 +237,8 @@ def tile_quantuminspiredneuralcore_pa_s_kernel(tc, x, amp_w, amp_b, ph_w, ph_b, 
         take_wave(0, nc.gpsimd)
         take_sine(1)
         take_wave(1, nc.gpsimd)
+        half_amp_bias = keep.tile([P, FEATURE_TILES], F32)
+        nc.scalar.mul(out=half_amp_bias[:], in_=bias_t[:, 0:FEATURE_TILES], mul=0.5)
         multiply_amp(0)
         take_sine(3)
         multiply_amp(1)

@@ -111,7 +111,8 @@ def tile_quantuminspiredneuralcore_pa_s_kernel(tc, x, amp_w, amp_b, ph_w, ph_b, 
             in_=ph_b.rearrange("(f c) -> f c", c=P),
         )
         load_weight(nc, ph_raw, ph_w, slice(HALF, FEATURES))
-        load_weight(nc, amp_raw, amp_w, slice(0, FEATURES))
+        load_weight(nc, amp_raw, amp_w, slice(0, HALF))
+        load_weight(nc, amp_raw, amp_w, slice(HALF, FEATURES))
 
         ident_f32 = keep.tile([P, P], F32)
         make_identity(nc, ident_f32[:])

@@ -93,6 +93,8 @@ def tile_quantuminspiredneuralcore_pa_s_kernel(tc, x, amp_w, amp_b, ph_w, ph_b, 
         banks = stack.enter_context(tc.psum_pool(name="banks", bufs=8))
         stack.enter_context(tc.manual_schedule())
 
+        zeros = keep.tile([P, P], F32)
+        nc.vector.memset(zeros[:], 0.0)
         x_sb = keep.tile([P, TOKEN_TILES, K], BF16)
         for a in range(TOKEN_TILES):
             nc.sync.dma_start(out=x_sb[:, a, :], in_=x_rows[:, a, :])
@@ -100,8 +102,6 @@ def tile_quantuminspiredneuralcore_pa_s_kernel(tc, x, amp_w, amp_b, ph_w, ph_b, 
         amp_raw = keep.tile([P, PACK, FEATURES], BF16)
         bias_rows = keep.tile([P, P], BF16)
         nc.vector.memset(bias_rows[:], 0.0)
-        zeros = keep.tile([P, P], F32)
-        nc.vector.memset(zeros[:], 0.0)
         load_weight(nc, ph_raw, ph_w, slice(0, HALF))
         nc.sync.dma_start(
             out=bias_rows[0:FEATURE_TILES, :], in_=amp_b.rearrange("(f c) -> f c", c=P)
@@ -162,12 +162,12 @@ def tile_quantuminspiredneuralcore_pa_s_kernel(tc, x, amp_w, amp_b, ph_w, ph_b, 
         quantise(nc, ph_op, tile_of(1))
         group(nc.vector.tensor_copy, ph_op, ph_raw, tile_of(2))
         quantise(nc, ph_op, tile_of(last))
-        group(nc.vector.tensor_copy, amp_op, amp_raw, tile_of(0))
+        halves = (slice(0, HALF), slice(HALF, FEATURES))
         quantise(nc, ph_op, tile_of(2))
-        for f in range(1, FEATURE_TILES):
-            group(nc.vector.tensor_copy, amp_op, amp_raw, tile_of(f))
-            quantise(nc, amp_op, tile_of(f - 1))
-        quantise(nc, amp_op, tile_of(last))
+        for cols in halves:
+            group(nc.vector.tensor_copy, amp_op, amp_raw, cols)
+        for cols in halves:
+            quantise(nc, amp_op, cols)
 
         tanh_ph = keep.tile([P, FEATURE_TILES, TOKENS], F32)
         tanh_amp = keep.tile([P, FEATURE_TILES, TOKENS], F32)
@@ -244,7 +244,7 @@ def tile_quantuminspiredneuralcore_pa_s_kernel(tc, x, amp_w, amp_b, ph_w, ph_b, 
         take_sine(3)
         multiply_amp(1)
         take_tanh(0, every)
-        take_wave(3, nc.vector)
+        take_wave(3, nc.gpsimd)
         take_sine(2)
         multiply_amp(2)
         multiply_amp(3)

@@ -151,18 +151,21 @@ def tile_quantuminspiredneuralcore_pa_s_kernel(tc, x, amp_w, amp_b, ph_w, ph_b, 
         amp_op = operand(keep, FEATURES, "amp")
         last = FEATURE_TILES - 1
         group(nc.scalar.copy, ph_op, ph_raw, tile_of(last))
-        ph_bias = keep.tile([P, FEATURE_TILES], F32)
-        nc.scalar.copy(out=ph_bias[:], in_=bias_t[:, FEATURE_TILES : 2 * FEATURE_TILES])
-        group(nc.vector.tensor_copy, ph_op, ph_raw, tile_of(0))
-        group(nc.vector.tensor_copy, ph_op, ph_raw, tile_of(1))
-        quantise(nc, ph_op, tile_of(0))
+        biases = keep.tile([P, 2 * FEATURE_TILES], F32)
+        nc.scalar.copy(out=biases[:], in_=bias_t[:, 0 : 2 * FEATURE_TILES])
+        ph_bias = biases[:, FEATURE_TILES : 2 * FEATURE_TILES]
+        half_amp_bias = keep.tile([P, FEATURE_TILES], F32)
+        nc.gpsimd.tensor_scalar(
+            out=half_amp_bias[:], in0=biases[:, 0:FEATURE_TILES], scalar1=0.5, scalar2=0.0, op0=ALU.mult, op1=ALU.add
+        )
+        halves = (slice(0, HALF), slice(HALF, FEATURES))
         x_parts = (slice(0, HALF), slice(HALF, TOKENS))
-        for tokens in x_parts:
-            quantise(nc, x_op, tokens)
-        quantise(nc, ph_op, tile_of(1))
+        group(nc.vector.tensor_copy, ph_op, ph_raw, halves[0])
+        for f in range(2):
+            quantise(nc, x_op, x_parts[f])
+            quantise(nc, ph_op, tile_of(f))
         group(nc.vector.tensor_copy, ph_op, ph_raw, tile_of(2))
         quantise(nc, ph_op, tile_of(last))
-        halves = (slice(0, HALF), slice(HALF, FEATURES))
         quantise(nc, ph_op, tile_of(2))
         for cols in halves:
             group(nc.vector.tensor_copy, amp_op, amp_raw, cols)
@@ -230,31 +233,28 @@ def tile_quantuminspiredneuralcore_pa_s_kernel(tc, x, amp_w, amp_b, ph_w, ph_b, 
             )
             nc.sync.dma_start(out=out_rows[:, part, tile_of(f)], in_=result[:, part, tile_of(f)])
 
-        turn_ph(0)
-        turn_ph(1)
-        turn_ph(3)
-        turn_ph(2)
+        order = (0, 1, 3, 2)
+        for f in order:
+            turn_ph(f)
         take_sine(0)
         take_wave(0, nc.gpsimd)
         take_sine(1)
         take_wave(1, nc.gpsimd)
-        half_amp_bias = keep.tile([P, FEATURE_TILES], F32)
-        nc.scalar.mul(out=half_amp_bias[:], in_=bias_t[:, 0:FEATURE_TILES], mul=0.5)
         multiply_amp(0)
         take_sine(3)
+        take_wave(3, nc.gpsimd)
         multiply_amp(1)
         take_tanh(0, every)
-        take_wave(3, nc.gpsimd)
         take_sine(2)
-        multiply_amp(2)
+        take_wave(2, nc.gpsimd)
         multiply_amp(3)
+        multiply_amp(2)
         take_tanh(1, every)
         finish(0, every)
-        take_wave(2, nc.vector)
-        take_tanh(2, every)
+        take_tanh(3, every)
         finish(1, every)
-        take_tanh(3, range(0, 2))
-        finish(2, every)
-        finish(3, range(0, 2))
-        take_tanh(3, range(2, TOKEN_TILES))
-        finish(3, range(2, TOKEN_TILES))
+        take_tanh(2, range(0, 2))
+        finish(3, every)
+        finish(2, range(0, 2))
+        take_tanh(2, range(2, TOKEN_TILES))
+        finish(2, range(2, TOKEN_TILES))

import math
from contextlib import ExitStack

import concourse.mybir as mybir
from concourse.masks import make_identity

F32 = mybir.dt.float32
BF16 = mybir.dt.bfloat16
U32 = mybir.dt.uint32
U8 = mybir.dt.uint8
FP8X4 = mybir.dt.float8_e4m3fn_x4
ACT = mybir.ActivationFunctionType
ALU = mybir.AluOpType

P = 128
PACK = 4
K = P * PACK
TOKENS = 384
TOKEN_TILES = TOKENS // P
FEATURES = 512
FEATURE_TILES = FEATURES // P
HALF = 256

FLOPS = 2 * TOKENS * K * 2 * FEATURES


def tile_of(f):
    return slice(f * P, (f + 1) * P)


def load_weight(nc, raw, weight, cols):
    nc.sync.dma_start(
        out=raw[:, :, cols], in_=weight.rearrange("(q t) n -> q t n", t=PACK)[:, :, cols]
    )


def quantise(nc, op, cols):
    grouped, codes, scales = op
    nc.vector.quantize_mx(
        out=codes[:, cols].bitcast(FP8X4),
        scales=scales[:, cols],
        in_=grouped[:, cols, :].rearrange("p c t -> p (c t)"),
    )


def group(copy, op, raw, cols):
    copy(
        out=op[0][:, cols, :].rearrange("p (c i) t -> p c t i", i=4),
        in_=raw[:, :, cols].rearrange("p t (c i) -> p c t i", i=4),
    )


def operand(pool, columns, name):
    grouped = pool.tile([P, columns, PACK], BF16, name=name + "_grouped", align_bytes=64)
    codes = pool.tile([P, columns], U32, name=name + "_codes", align_bytes=64)
    scales = pool.tile([P, columns], U8, name=name + "_scales", align_bytes=64)
    return grouped, codes, scales


def multiply(nc, out, w, x, f, tokens):
    nc.tensor.matmul_mx(
        out=out,
        lhsT=w[1][:, tile_of(f)].bitcast(FP8X4),
        lhsT_scale=w[2][:, tile_of(f)],
        rhs=x[1][:, tokens].bitcast(FP8X4),
        rhs_scale=x[2][:, tokens],
        start=True,
        stop=True,
    )


def multiply_all(nc, banks, w, x, f, name):
    product = banks.tile([P, TOKENS], F32, tag="bank", name=name)
    for tokens in (slice(0, HALF), slice(HALF, TOKENS)):
        multiply(nc, product[:, tokens], w, x, f, tokens)
    return product


def to_token_rows(nc, banks, values, ident, tiles, name):
    rows = banks.tile([P, len(tiles), P], F32, tag="bank", name=name)
    for i in range(len(tiles)):
        nc.tensor.transpose(rows[:, i, :], values[:, tile_of(tiles[i])], ident[:])
    return rows


def tile_quantuminspiredneuralcore_pa_s_kernel(tc, x, amp_w, amp_b, ph_w, ph_b, out):
    nc = tc.nc
    x_rows = x.flatten_outer_dims().rearrange("(p a) k -> p a k", a=TOKEN_TILES)
    out_rows = out.flatten_outer_dims().rearrange("(p a) n -> p a n", a=TOKEN_TILES)

    with ExitStack() as stack:
        keep = stack.enter_context(tc.tile_pool(name="keep", bufs=1))
        banks = stack.enter_context(tc.psum_pool(name="banks", bufs=8))
        stack.enter_context(tc.manual_schedule())

        zeros = keep.tile([P, P], F32)
        nc.vector.memset(zeros[:], 0.0)
        x_sb = keep.tile([P, TOKEN_TILES, K], BF16)
        for a in range(TOKEN_TILES):
            nc.sync.dma_start(out=x_sb[:, a, :], in_=x_rows[:, a, :])
        ph_raw = keep.tile([P, PACK, FEATURES], BF16)
        amp_raw = keep.tile([P, PACK, FEATURES], BF16)
        bias_rows = keep.tile([P, P], BF16)
        nc.vector.memset(bias_rows[:], 0.0)
        load_weight(nc, ph_raw, ph_w, slice(0, HALF))
        nc.sync.dma_start(
            out=bias_rows[0:FEATURE_TILES, :], in_=amp_b.rearrange("(f c) -> f c", c=P)
        )
        nc.sync.dma_start(
            out=bias_rows[FEATURE_TILES : 2 * FEATURE_TILES, :],
            in_=ph_b.rearrange("(f c) -> f c", c=P),
        )
        load_weight(nc, ph_raw, ph_w, slice(HALF, FEATURES))
        load_weight(nc, amp_raw, amp_w, slice(0, HALF))
        load_weight(nc, amp_raw, amp_w, slice(HALF, FEATURES))

        ident_f32 = keep.tile([P, P], F32)
        make_identity(nc, ident_f32[:])
        ident_bf16 = keep.tile([P, P], BF16)
        make_identity(nc, ident_bf16[:])
        one = keep.tile([P, 1], F32)
        nc.vector.memset(one[:], 1.0)
        unused = keep.tile([P, 1], F32)
        nc.scalar.activation(out=unused[:], in_=one[:], func=ACT.Silu)

        idle = banks.tile([P, P], F32, tag="bank", name="idle")

        def keep_warm(count, columns):
            for i in range(count):
                nc.tensor.matmul(idle[:, 0:columns], lhsT=zeros[:], rhs=zeros[:, 0:columns], start=True, stop=True)

        keep_warm(3, 128)

        x_words = x_sb[:].bitcast(F32).rearrange("p a (q u) -> p a u q", u=2)
        x_op = operand(keep, TOKENS, "x")
        x_grouped_words = x_op[0][:].bitcast(F32)
        for a in range(TOKEN_TILES):
            x_t = banks.tile([P, 2, P], F32, tag="bank", name="x_t")
            for u in range(2):
                nc.tensor.transpose(x_t[:, u, :], x_words[:, a, u, :], ident_f32[:])
            nc.scalar.copy(
                out=x_grouped_words[:, tile_of(a), :], in_=x_t[:].rearrange("q u c -> q c u")
            )

        keep_warm(3, 64)

        bias_t = banks.tile([P, P], BF16, tag="bank", name="bias_t")
        nc.tensor.transpose(bias_t[:], bias_rows[:], ident_bf16[:])

        ph_op = operand(keep, FEATURES, "ph")
        amp_op = operand(keep, FEATURES, "amp")
        last = FEATURE_TILES - 1
        group(nc.scalar.copy, ph_op, ph_raw, tile_of(last))
        biases = keep.tile([P, 2 * FEATURE_TILES], F32)
        nc.scalar.copy(out=biases[:], in_=bias_t[:, 0 : 2 * FEATURE_TILES])
        ph_bias = biases[:, FEATURE_TILES : 2 * FEATURE_TILES]
        half_amp_bias = keep.tile([P, FEATURE_TILES], F32)
        nc.gpsimd.tensor_scalar(
            out=half_amp_bias[:], in0=biases[:, 0:FEATURE_TILES], scalar1=0.5, scalar2=0.0, op0=ALU.mult, op1=ALU.add
        )
        halves = (slice(0, HALF), slice(HALF, FEATURES))
        x_parts = (slice(0, HALF), slice(HALF, TOKENS))
        group(nc.vector.tensor_copy, ph_op, ph_raw, halves[0])
        for f in range(2):
            quantise(nc, x_op, x_parts[f])
            quantise(nc, ph_op, tile_of(f))
        group(nc.vector.tensor_copy, ph_op, ph_raw, tile_of(2))
        quantise(nc, ph_op, tile_of(last))
        quantise(nc, ph_op, tile_of(2))
        for cols in halves:
            group(nc.vector.tensor_copy, amp_op, amp_raw, cols)
        for cols in halves:
            quantise(nc, amp_op, cols)

        tanh_ph = keep.tile([P, FEATURE_TILES, TOKENS], F32)
        tanh_amp = keep.tile([P, FEATURE_TILES, TOKENS], F32)
        sine = keep.tile([P, FEATURE_TILES, TOKEN_TILES, P], F32)
        square = keep.tile([P, FEATURE_TILES, TOKEN_TILES, P], F32)
        wave = keep.tile([P, FEATURE_TILES, TOKEN_TILES, P], F32)
        result = keep.tile([P, TOKEN_TILES, FEATURES], F32)

        for tokens in x_parts:
            product = banks.tile([P, HALF], F32, tag="bank", name="ph_part")
            columns = tokens.stop - tokens.start
            multiply(nc, product[:, 0:columns], ph_op, x_op, 0, tokens)
            nc.scalar.activation(
                out=tanh_ph[:, 0, tokens], in_=product[:, 0:columns], func=ACT.Tanh, bias=ph_bias[:, 0:1]
            )
        for f in (1, 3, 2):
            product = multiply_all(nc, banks, ph_op, x_op, f, "ph_product")
            nc.scalar.activation(
                out=tanh_ph[:, f, :], in_=product[:], func=ACT.Tanh, bias=ph_bias[:, f : f + 1]
            )

        every = range(TOKEN_TILES)
        ph_rows = {}
        products = {}

        def turn_ph(f):
            ph_rows[f] = to_token_rows(nc, banks, tanh_ph[:, f, :], ident_f32, every, "tanh_ph_t")

        def take_sine(f):
            nc.scalar.activation(
                out=sine[:, f], in_=ph_rows[f][:], func=ACT.Sin, scale=0.5 * math.pi, bias=-0.125 * math.pi
            )
            nc.vector.scalar_tensor_tensor(
                out=square[:, f], in0=sine[:, f], scalar=math.sqrt(2.0), in1=sine[:, f], op0=ALU.mult, op1=ALU.mult
            )

        def take_wave(f, engine):
            engine.tensor_scalar(
                out=wave[:, f], in0=square[:, f], scalar1=-1.0, scalar2=1.0 / math.sqrt(2.0), op0=ALU.mult, op1=ALU.add
            )

        def multiply_amp(f):
            products[f] = multiply_all(nc, banks, amp_op, x_op, f, "amp_product")

        def take_tanh(f, tiles):
            tokens = slice(tiles[0] * P, (tiles[-1] + 1) * P)
            nc.scalar.activation(
                out=tanh_amp[:, f, tokens],
                in_=products[f][:, tokens],
                func=ACT.Tanh,
                bias=half_amp_bias[:, f : f + 1],
                scale=0.5,
            )

        def finish(f, tiles):
            part = slice(tiles[0], tiles[-1] + 1)
            rows = to_token_rows(nc, banks, tanh_amp[:, f, :], ident_f32, tiles, "tanh_amp_t")
            nc.vector.scalar_tensor_tensor(
                out=result[:, part, tile_of(f)], in0=rows[:], scalar=1.0, in1=wave[:, f, part, :], op0=ALU.add, op1=ALU.mult
            )
            nc.sync.dma_start(out=out_rows[:, part, tile_of(f)], in_=result[:, part, tile_of(f)])

        order = (0, 1, 3, 2)
        for f in order:
            turn_ph(f)
        take_sine(0)
        take_wave(0, nc.gpsimd)
        take_sine(1)
        take_wave(1, nc.gpsimd)
        multiply_amp(0)
        take_sine(3)
        take_wave(3, nc.gpsimd)
        multiply_amp(1)
        take_tanh(0, every)
        take_sine(2)
        take_wave(2, nc.gpsimd)
        multiply_amp(3)
        multiply_amp(2)
        take_tanh(1, every)
        finish(0, every)
        take_tanh(3, every)
        finish(1, every)
        take_tanh(2, range(0, 2))
        finish(3, every)
        finish(2, range(0, 2))
        take_tanh(2, range(2, TOKEN_TILES))
        finish(2, range(2, TOKEN_TILES))
